import numpy as np
import ml_dtypes


def mxq(x, axis, fmt="e4m3"):
    dtype, down = {"e4m3": (ml_dtypes.float8_e4m3fn, 7), "e5m2": (ml_dtypes.float8_e5m2, 14)}[fmt]
    v = np.moveaxis(np.asarray(x, np.float32).astype(ml_dtypes.bfloat16).astype(np.float64), axis, -1)
    blocks = v.reshape(v.shape[:-1] + (-1, 32))
    amax = np.abs(blocks).max(-1, keepdims=True)
    byte = np.maximum(np.where(amax > 0, np.frexp(amax)[1] - 1 + 127, 0) - down, 1)
    scale = np.exp2(byte - 127.0)
    codes = (blocks / scale).astype(np.float32).astype(dtype).astype(np.float64)
    return np.moveaxis((codes * scale).reshape(v.shape), -1, axis)


WIDE = False


def mx_kscale(k):
    if not WIDE:
        return np.ones(k)
    levels = np.array([10, -10, 5, -5, 0])
    a = np.random.permutation(np.resize(levels, k // 512 * 4)).reshape(k // 512, 4)
    idx = np.arange(k)
    return np.exp2(a[idx // 512, idx % 128 // 32])


BF16 = ml_dtypes.bfloat16


def bf(x):
    return np.asarray(x, np.float32).astype(BF16)


def f64(x):
    return np.asarray(x).astype(np.float64)


B, CH, C1, C2, D, NF, W, H = 1, 1024, 128, 512, 2, 8, 16, 16
N = NF * W * H
M = NF * (W // D) * (H // D)


def conv(xq, w, b):
    return (mxq(f64(w), 1, "e4m3") @ xq) + f64(b)[None, :, None]


def maxpool_wh(v):
    return v.reshape(B, -1, NF, W // D, D, H // D, D).max(axis=(4, 6)).reshape(B, -1, M)


def setup_inputs():
    s = mx_kscale(CH)
    return {"x": bf(np.random.standard_normal((B, CH, NF, W, H)) * s[None, :, None, None, None]),
            "w_theta": bf(np.random.standard_normal((C1, CH)) * 0.3 / np.sqrt(CH) / s),
            "b_theta": bf(np.random.standard_normal(C1) * 0.1),
            "w_phi": bf(np.random.standard_normal((C1, CH)) * 0.3 / np.sqrt(CH) / s),
            "b_phi": bf(np.random.standard_normal(C1) * 0.1),
            "w_g": bf(np.random.standard_normal((C2, CH)) / np.sqrt(CH) / s),
            "b_g": bf(np.random.standard_normal(C2) * 0.2)}


def reference(x, w_theta, b_theta, w_phi, b_phi, w_g, b_g):
    xq = mxq(f64(x).reshape(B, CH, N), 1, "e4m3")
    theta = np.tanh(conv(xq, w_theta, b_theta)).transpose(0, 2, 1)
    phi = maxpool_wh(np.tanh(conv(xq, w_phi, b_phi))).transpose(0, 2, 1)
    g = maxpool_wh(conv(xq, w_g, b_g)).transpose(0, 2, 1)
    return theta, phi, g

@@ -1,0 +1,246 @@
+from contextlib import ExitStack
+
+import concourse.mybir as mybir
+from concourse.masks import make_identity
+
+FLOPS = 2 * (128 + 128 + 512) * 1024 * 2048
+
+BF16 = mybir.dt.bfloat16
+F32 = mybir.dt.float32
+U32 = mybir.dt.uint32
+U8 = mybir.dt.uint8
+FP8X4 = mybir.dt.float8_e4m3fn_x4
+ALU = mybir.AluOpType
+ACT = mybir.ActivationFunctionType
+
+P = 128
+PACK = 4
+PASSES = 2
+HALVES = 2
+PAIR = 2
+CHANNELS = 1024
+CHUNKS = 4
+CHUNK = 512
+WINDOW_ROWS = 16
+WINDOW_COLS = 8
+MEMBERS = 4
+C_G = 512
+C_PHI = 128
+C_THETA = 128
+BANK = 512
+PSUM_BANKS = 8
+
+
+def tile_selfattention3d_pb_kernel(
+    tc, x, w_theta, b_theta, w_phi, b_phi, w_g, b_g, out_0, out_1, out_2
+):
+    nc = tc.nc
+
+    x_pieces = x.rearrange(
+        "o (s p e) f i j -> (o s) p e (f i j)", s=PASSES * HALVES, p=P, e=PAIR
+    )
+    theta_rows = out_0.rearrange(
+        "o (t a di b dj) c -> (o t) b a di (dj c)",
+        t=CHUNKS, a=WINDOW_ROWS, di=2, b=WINDOW_COLS, dj=2,
+    )
+    phi_rows = out_1.rearrange("o (t w) c -> (o t) w c", t=CHUNKS)
+    g_rows = out_2.rearrange("o (t w) c -> (o t) w c", t=CHUNKS)
+
+    with ExitStack() as ctx:
+        consts = ctx.enter_context(tc.tile_pool(name="consts", bufs=1))
+        raw_pool = ctx.enter_context(tc.tile_pool(name="raw", bufs=CHUNKS))
+        grouped_pool = ctx.enter_context(tc.tile_pool(name="grouped", bufs=3))
+        quantised_pool = ctx.enter_context(tc.tile_pool(name="quantised", bufs=2))
+        results = ctx.enter_context(tc.tile_pool(name="results", bufs=2))
+        psum = ctx.enter_context(tc.psum_pool(name="psum", bufs=PSUM_BANKS))
+
+        def load_chunk(t):
+            raw = raw_pool.tile([P, PASSES, PACK, CHUNK], BF16)
+            for c in range(PASSES):
+                for u in range(HALVES):
+                    nc.sync.dma_start(
+                        out=raw[:, c, PAIR * u : PAIR * (u + 1), :],
+                        in_=x_pieces[HALVES * c + u, :, :, t * CHUNK : (t + 1) * CHUNK],
+                    )
+            return raw
+
+        w_rows = consts.tile([P, 6, CHANNELS], BF16)
+        raws = [load_chunk(0)]
+        nc.sync.dma_start(out=w_rows[:, 4, :], in_=w_phi)
+        nc.sync.dma_start(out=w_rows[:, 5, :], in_=w_theta)
+        nc.sync.dma_start(out=w_rows[:, 0:4, :], in_=w_g.rearrange("(r p) k -> p r k", p=P))
+        for t in range(1, CHUNKS):
+            raws.append(load_chunk(t))
+
+        warm = consts.tile([P, 1], F32)
+        nc.vector.memset(warm[:], 0.0)
+        nc.scalar.activation(out=warm[:], in_=warm[:], func=ACT.Tanh)
+
+        ident = consts.tile([P, P], F32)
+        make_identity(nc, ident[:])
+
+        bias_rows = consts.tile([P, C_G + C_PHI + C_THETA], BF16)
+        nc.vector.memset(bias_rows[:], 0.0)
+        nc.scalar.dma_start(out=bias_rows[0:1, 0:C_G], in_=b_g.rearrange("(o n) -> o n", o=1))
+        nc.scalar.dma_start(
+            out=bias_rows[0:1, C_G : C_G + C_PHI], in_=b_phi.rearrange("(o n) -> o n", o=1)
+        )
+        nc.scalar.dma_start(
+            out=bias_rows[0:1, C_G + C_PHI :], in_=b_theta.rearrange("(o n) -> o n", o=1)
+        )
+        ones = consts.tile([P, P], BF16)
+        nc.vector.memset(ones[:], 1.0)
+        bias = consts.tile([P, C_G + C_PHI + C_THETA], F32)
+        for first, width in ((0, C_G), (C_G, C_PHI + C_THETA)):
+            bias_bank = psum.tile([P, BANK], F32, tag="bank")
+            nc.tensor.matmul(
+                out=bias_bank[:, 0:width],
+                lhsT=ones[:],
+                rhs=bias_rows[:, first : first + width],
+                start=True,
+                stop=True,
+            )
+            nc.scalar.copy(out=bias[:, first : first + width], in_=bias_bank[:, 0:width])
+        bias_theta = bias[:, C_G + C_PHI :].unsqueeze(1).to_broadcast([P, MEMBERS, C_THETA])
+
+        def regroup(t):
+            grouped = grouped_pool.tile([P, PASSES, MEMBERS, P, PACK], BF16, align_bytes=64)
+            for c in range(PASSES):
+                for di in range(2):
+                    if c == 0 and di == 0:
+                        nc.vector.tensor_copy(
+                            out=grouped[:, c, 2 * di : 2 * di + 2, :, :].rearrange(
+                                "p dj (a b) k -> p a b k dj", a=WINDOW_ROWS
+                            ),
+                            in_=raws[t][:, c, :, :].rearrange(
+                                "p k (a di b dj) -> p di a b k dj",
+                                a=WINDOW_ROWS, di=2, b=WINDOW_COLS, dj=2,
+                            )[:, di],
+                        )
+                    else:
+                        for dj in range(2):
+                            nc.scalar.copy(
+                                out=grouped[:, c, 2 * di + dj, :, :].rearrange(
+                                    "p (a b) k -> p a b k", a=WINDOW_ROWS
+                                ),
+                                in_=raws[t][:, c, :, :].rearrange(
+                                    "p k (a di b dj) -> p di dj a b k",
+                                    a=WINDOW_ROWS, di=2, b=WINDOW_COLS, dj=2,
+                                )[:, di, dj],
+                            )
+            return grouped
+
+        def quantise(grouped):
+            codes = quantised_pool.tile([P, PASSES, MEMBERS, P], U32, align_bytes=64)
+            scales = quantised_pool.tile([P, PASSES, MEMBERS, P], U8, align_bytes=64)
+            nc.vector.quantize_mx(
+                out=codes[:].rearrange("p c m w -> p (c m w)").bitcast(FP8X4),
+                scales=scales[:].rearrange("p c m w -> p (c m w)"),
+                in_=grouped[:].rearrange("p c m w k -> p (c m w k)"),
+            )
+            return codes, scales
+
+        def quantise_weights(first_row_tile, row_tiles):
+            columns = row_tiles * P
+            grouped = consts.tile(
+                [P, PASSES, columns * PACK], BF16, align_bytes=64, name="w_grouped%d" % first_row_tile
+            )
+            for c in range(PASSES):
+                for pair in range(row_tiles // 2):
+                    w_bank = psum.tile([P, 2, HALVES, P], F32, tag="bank")
+                    for r in range(2):
+                        words = w_rows[:, first_row_tile + 2 * pair + r, :].bitcast(F32)
+                        for u in range(HALVES):
+                            first = (HALVES * c + u) * P
+                            nc.tensor.transpose(
+                                w_bank[:, r, u, :], words[:, first : first + P], ident[:]
+                            )
+                    out_words = grouped[:, c, :].bitcast(F32)[
+                        :, pair * BANK : (pair + 1) * BANK
+                    ].rearrange("p (r o u) -> p r o u", r=2, u=HALVES)
+                    in_words = w_bank[:].rearrange("p r u o -> p r o u")
+                    if c == 0:
+                        nc.scalar.copy(out=out_words, in_=in_words)
+                    else:
+                        nc.vector.tensor_copy(out=out_words, in_=in_words)
+            codes = consts.tile(
+                [P, PASSES, columns], U32, align_bytes=64, name="w_codes%d" % first_row_tile
+            )
+            scales = consts.tile(
+                [P, PASSES, columns], U8, align_bytes=64, name="w_scales%d" % first_row_tile
+            )
+            nc.vector.quantize_mx(
+                out=codes[:].rearrange("p c n -> p (c n)").bitcast(FP8X4),
+                scales=scales[:].rearrange("p c n -> p (c n)"),
+                in_=grouped[:].rearrange("p c n -> p (c n)"),
+            )
+            return codes, scales
+
+        def product(out, x_codes, x_scales, member, w_codes, w_scales, first, width):
+            for c in range(PASSES):
+                nc.tensor.matmul_mx(
+                    out=out,
+                    lhsT=x_codes[:, c, member, :].bitcast(FP8X4),
+                    lhsT_scale=x_scales[:, c, member, :],
+                    rhs=w_codes[:, c, first : first + width].bitcast(FP8X4),
+                    rhs_scale=w_scales[:, c, first : first + width],
+                    start=(c == 0),
+                    stop=(c == PASSES - 1),
+                )
+
+        def convolve_pool_store(t, x_codes, x_scales):
+            theta_bank = psum.tile([P, MEMBERS, C_THETA], F32, tag="bank")
+            for member in range(MEMBERS):
+                product(theta_bank[:, member, :], x_codes, x_scales, member,
+                        small_codes, small_scales, C_PHI, C_THETA)
+            phi_bank = psum.tile([P, MEMBERS, C_PHI], F32, tag="bank")
+            for member in range(MEMBERS):
+                product(phi_bank[:, member, :], x_codes, x_scales, member,
+                        small_codes, small_scales, 0, C_PHI)
+
+            theta = results.tile([P, MEMBERS, C_THETA], F32)
+            nc.vector.tensor_tensor(out=theta[:], in0=theta_bank[:], in1=bias_theta, op=ALU.add)
+            nc.scalar.activation(out=theta[:], in_=theta[:], func=ACT.Tanh)
+            for b in range(WINDOW_COLS):
+                nc.sync.dma_start(
+                    out=theta_rows[t, b],
+                    in_=theta[b:P:WINDOW_COLS, :, :].rearrange("a (di dj) c -> a di (dj c)", di=2),
+                )
+
+            pooled = results.tile([P, C_G + C_PHI], F32)
+            phi_halves = results.tile([P, 2, C_PHI], F32)
+            nc.scalar.copy(out=phi_halves[:], in_=phi_bank[:, 0:2, :])
+            nc.vector.tensor_tensor(
+                out=phi_halves[:], in0=phi_bank[:, 2:4, :], in1=phi_halves[:], op=ALU.max
+            )
+            for member in range(MEMBERS):
+                g_bank = psum.tile([P, C_G], F32, tag="bank")
+                product(g_bank[:], x_codes, x_scales, member, g_codes, g_scales, 0, C_G)
+                if member == 0:
+                    nc.scalar.copy(out=pooled[:, 0:C_G], in_=g_bank[:])
+                else:
+                    nc.vector.tensor_tensor(
+                        out=pooled[:, 0:C_G], in0=g_bank[:], in1=pooled[:, 0:C_G], op=ALU.max
+                    )
+            nc.vector.tensor_tensor(
+                out=pooled[:, C_G:], in0=phi_halves[:, 0, :], in1=phi_halves[:, 1, :], op=ALU.max
+            )
+            nc.vector.tensor_tensor(
+                out=pooled[:], in0=pooled[:], in1=bias[:, 0 : C_G + C_PHI], op=ALU.add
+            )
+            nc.sync.dma_start(out=g_rows[t], in_=pooled[:, 0:C_G])
+            phi = results.tile([P, C_PHI], F32)
+            nc.scalar.activation(out=phi[:], in_=pooled[:, C_G:], func=ACT.Tanh)
+            nc.sync.dma_start(out=phi_rows[t], in_=phi[:])
+
+        groupeds = [regroup(0)]
+        small_codes, small_scales = quantise_weights(4, 2)
+        g_codes, g_scales = quantise_weights(0, 4)
+        groupeds.append(regroup(1))
+        quantised = [quantise(groupeds[0])]
+        for t in range(CHUNKS):
+            if t + 2 < CHUNKS:
+                groupeds.append(regroup(t + 2))
+            if t + 1 < CHUNKS:
+                quantised.append(quantise(groupeds[t + 1]))
+            convolve_pool_store(t, quantised[t][0], quantised[t][1])

@@ -27,6 +27,7 @@ MEMBERS = 4
 C_G = 512
 C_PHI = 128
 C_THETA = 128
+BLOCK = 256
 BANK = 512
 PSUM_BANKS = 8
 
@@ -45,32 +46,44 @@ def tile_selfattention3d_pb_kernel(
     )
     phi_rows = out_1.rearrange("o (t w) c -> (o t) w c", t=CHUNKS)
     g_rows = out_2.rearrange("o (t w) c -> (o t) w c", t=CHUNKS)
+    w_g_tiles = w_g.rearrange("(r p) k -> p r k", p=P)
 
     with ExitStack() as ctx:
         consts = ctx.enter_context(tc.tile_pool(name="consts", bufs=1))
-        raw_pool = ctx.enter_context(tc.tile_pool(name="raw", bufs=CHUNKS))
-        grouped_pool = ctx.enter_context(tc.tile_pool(name="grouped", bufs=3))
-        quantised_pool = ctx.enter_context(tc.tile_pool(name="quantised", bufs=2))
-        results = ctx.enter_context(tc.tile_pool(name="results", bufs=2))
+        per_chunk = ctx.enter_context(tc.tile_pool(name="per_chunk", bufs=CHUNKS))
+        results = ctx.enter_context(tc.tile_pool(name="results", bufs=CHUNKS))
         psum = ctx.enter_context(tc.psum_pool(name="psum", bufs=PSUM_BANKS))
 
+        raws = [per_chunk.tile([P, PASSES, PACK, CHUNK], BF16, name="raw") for t in range(CHUNKS)]
+        groupeds = [
+            per_chunk.tile([P, PASSES, MEMBERS, P, PACK], BF16, align_bytes=64, name="grouped")
+            for t in range(CHUNKS)
+        ]
+        x_codes = [
+            per_chunk.tile([P, PASSES, MEMBERS, P], U32, align_bytes=64, name="x_codes")
+            for t in range(CHUNKS)
+        ]
+        x_scales = [
+            per_chunk.tile([P, PASSES, MEMBERS, P], U8, align_bytes=64, name="x_scales")
+            for t in range(CHUNKS)
+        ]
+
         def load_chunk(t):
-            raw = raw_pool.tile([P, PASSES, PACK, CHUNK], BF16)
             for c in range(PASSES):
                 for u in range(HALVES):
                     nc.sync.dma_start(
-                        out=raw[:, c, PAIR * u : PAIR * (u + 1), :],
+                        out=raws[t][:, c, PAIR * u : PAIR * (u + 1), :],
                         in_=x_pieces[HALVES * c + u, :, :, t * CHUNK : (t + 1) * CHUNK],
                     )
-            return raw
 
         w_rows = consts.tile([P, 6, CHANNELS], BF16)
-        raws = [load_chunk(0)]
+        load_chunk(0)
         nc.sync.dma_start(out=w_rows[:, 4, :], in_=w_phi)
         nc.sync.dma_start(out=w_rows[:, 5, :], in_=w_theta)
-        nc.sync.dma_start(out=w_rows[:, 0:4, :], in_=w_g.rearrange("(r p) k -> p r k", p=P))
+        nc.sync.dma_start(out=w_rows[:, 0:2, :], in_=w_g_tiles[:, 0:2, :])
+        nc.sync.dma_start(out=w_rows[:, 2:4, :], in_=w_g_tiles[:, 2:4, :])
         for t in range(1, CHUNKS):
-            raws.append(load_chunk(t))
+            load_chunk(t)
 
         warm = consts.tile([P, 1], F32)
         nc.vector.memset(warm[:], 0.0)
@@ -103,71 +116,66 @@ def tile_selfattention3d_pb_kernel(
             nc.scalar.copy(out=bias[:, first : first + width], in_=bias_bank[:, 0:width])
         bias_theta = bias[:, C_G + C_PHI :].unsqueeze(1).to_broadcast([P, MEMBERS, C_THETA])
 
-        def regroup(t):
-            grouped = grouped_pool.tile([P, PASSES, MEMBERS, P, PACK], BF16, align_bytes=64)
-            for c in range(PASSES):
-                for di in range(2):
-                    if c == 0 and di == 0:
-                        nc.vector.tensor_copy(
-                            out=grouped[:, c, 2 * di : 2 * di + 2, :, :].rearrange(
-                                "p dj (a b) k -> p a b k dj", a=WINDOW_ROWS
+        def regroup(q):
+            t, c = divmod(q, PASSES)
+            if t >= CHUNKS:
+                return
+            by_member = raws[t][:, c, :, :].rearrange(
+                "p k (a di b dj) -> p di dj a b k", a=WINDOW_ROWS, di=2, b=WINDOW_COLS, dj=2
+            )
+            for di in range(2):
+                if di == 0:
+                    nc.vector.tensor_copy(
+                        out=groupeds[t][:, c, 0:2, :, :].rearrange(
+                            "p dj (a b) k -> p a b k dj", a=WINDOW_ROWS
+                        ),
+                        in_=raws[t][:, c, :, :].rearrange(
+                            "p k (a di b dj) -> p di a b k dj",
+                            a=WINDOW_ROWS, di=2, b=WINDOW_COLS, dj=2,
+                        )[:, 0],
+                    )
+                else:
+                    for dj in range(2):
+                        nc.scalar.copy(
+                            out=groupeds[t][:, c, 2 * di + dj, :, :].rearrange(
+                                "p (a b) k -> p a b k", a=WINDOW_ROWS
                             ),
-                            in_=raws[t][:, c, :, :].rearrange(
-                                "p k (a di b dj) -> p di a b k dj",
-                                a=WINDOW_ROWS, di=2, b=WINDOW_COLS, dj=2,
-                            )[:, di],
+                            in_=by_member[:, di, dj],
                         )
-                    else:
-                        for dj in range(2):
-                            nc.scalar.copy(
-                                out=grouped[:, c, 2 * di + dj, :, :].rearrange(
-                                    "p (a b) k -> p a b k", a=WINDOW_ROWS
-                                ),
-                                in_=raws[t][:, c, :, :].rearrange(
-                                    "p k (a di b dj) -> p di dj a b k",
-                                    a=WINDOW_ROWS, di=2, b=WINDOW_COLS, dj=2,
-                                )[:, di, dj],
-                            )
-            return grouped
 
-        def quantise(grouped):
-            codes = quantised_pool.tile([P, PASSES, MEMBERS, P], U32, align_bytes=64)
-            scales = quantised_pool.tile([P, PASSES, MEMBERS, P], U8, align_bytes=64)
+        def quantise(t, c):
+            if t >= CHUNKS:
+                return
             nc.vector.quantize_mx(
-                out=codes[:].rearrange("p c m w -> p (c m w)").bitcast(FP8X4),
-                scales=scales[:].rearrange("p c m w -> p (c m w)"),
-                in_=grouped[:].rearrange("p c m w k -> p (c m w k)"),
+                out=x_codes[t][:, c, :, :].rearrange("p m w -> p (m w)").bitcast(FP8X4),
+                scales=x_scales[t][:, c, :, :].rearrange("p m w -> p (m w)"),
+                in_=groupeds[t][:, c, :, :, :].rearrange("p m w k -> p (m w k)"),
             )
-            return codes, scales
 
-        def quantise_weights(first_row_tile, row_tiles):
-            columns = row_tiles * P
+        def prepare_weights(first_row_tile):
             grouped = consts.tile(
-                [P, PASSES, columns * PACK], BF16, align_bytes=64, name="w_grouped%d" % first_row_tile
+                [P, PASSES, BLOCK * PACK], BF16, align_bytes=64,
+                name="w_grouped%d" % first_row_tile,
             )
             for c in range(PASSES):
-                for pair in range(row_tiles // 2):
-                    w_bank = psum.tile([P, 2, HALVES, P], F32, tag="bank")
-                    for r in range(2):
-                        words = w_rows[:, first_row_tile + 2 * pair + r, :].bitcast(F32)
-                        for u in range(HALVES):
-                            first = (HALVES * c + u) * P
-                            nc.tensor.transpose(
-                                w_bank[:, r, u, :], words[:, first : first + P], ident[:]
-                            )
-                    out_words = grouped[:, c, :].bitcast(F32)[
-                        :, pair * BANK : (pair + 1) * BANK
-                    ].rearrange("p (r o u) -> p r o u", r=2, u=HALVES)
-                    in_words = w_bank[:].rearrange("p r u o -> p r o u")
-                    if c == 0:
-                        nc.scalar.copy(out=out_words, in_=in_words)
-                    else:
-                        nc.vector.tensor_copy(out=out_words, in_=in_words)
+                w_bank = psum.tile([P, 2, HALVES, P], F32, tag="bank")
+                for r in range(2):
+                    words = w_rows[:, first_row_tile + r, :].bitcast(F32)
+                    for u in range(HALVES):
+                        first = (HALVES * c + u) * P
+                        nc.tensor.transpose(
+                            w_bank[:, r, u, :], words[:, first : first + P], ident[:]
+                        )
+                out_words = grouped[:, c, :].bitcast(F32).rearrange(
+                    "p (r o u) -> p r o u", r=2, u=HALVES
+                )
+                in_words = w_bank[:].rearrange("p r u o -> p r o u")
+                nc.scalar.copy(out=out_words, in_=in_words)
             codes = consts.tile(
-                [P, PASSES, columns], U32, align_bytes=64, name="w_codes%d" % first_row_tile
+                [P, PASSES, BLOCK], U32, align_bytes=64, name="w_codes%d" % first_row_tile
             )
             scales = consts.tile(
-                [P, PASSES, columns], U8, align_bytes=64, name="w_scales%d" % first_row_tile
+                [P, PASSES, BLOCK], U8, align_bytes=64, name="w_scales%d" % first_row_tile
             )
             nc.vector.quantize_mx(
                 out=codes[:].rearrange("p c n -> p (c n)").bitcast(FP8X4),
@@ -176,30 +184,57 @@ def tile_selfattention3d_pb_kernel(
             )
             return codes, scales
 
-        def product(out, x_codes, x_scales, member, w_codes, w_scales, first, width):
+        def product(out, t, member, weights, first, width):
+            w_codes, w_scales = weights
             for c in range(PASSES):
                 nc.tensor.matmul_mx(
                     out=out,
-                    lhsT=x_codes[:, c, member, :].bitcast(FP8X4),
-                    lhsT_scale=x_scales[:, c, member, :],
+                    lhsT=x_codes[t][:, c, member, :].bitcast(FP8X4),
+                    lhsT_scale=x_scales[t][:, c, member, :],
                     rhs=w_codes[:, c, first : first + width].bitcast(FP8X4),
                     rhs_scale=w_scales[:, c, first : first + width],
                     start=(c == 0),
                     stop=(c == PASSES - 1),
                 )
 
-        def convolve_pool_store(t, x_codes, x_scales):
+        theta_banks = {}
+        phi_banks = {}
+        g_banks = {}
+
+        def products(t):
+            if t >= CHUNKS:
+                return
             theta_bank = psum.tile([P, MEMBERS, C_THETA], F32, tag="bank")
             for member in range(MEMBERS):
-                product(theta_bank[:, member, :], x_codes, x_scales, member,
-                        small_codes, small_scales, C_PHI, C_THETA)
+                product(theta_bank[:, member, :], t, member, w_small, C_PHI, C_THETA)
+            theta_banks[t] = theta_bank
             phi_bank = psum.tile([P, MEMBERS, C_PHI], F32, tag="bank")
             for member in range(MEMBERS):
-                product(phi_bank[:, member, :], x_codes, x_scales, member,
-                        small_codes, small_scales, 0, C_PHI)
+                product(phi_bank[:, member, :], t, member, w_small, 0, C_PHI)
+            phi_banks[t] = phi_bank
+            for member in range(MEMBERS):
+                g_bank = psum.tile([P, C_G], F32, tag="bank")
+                product(g_bank[:, 0:BLOCK], t, member, w_g_low, 0, BLOCK)
+                product(g_bank[:, BLOCK:C_G], t, member, w_g_high, 0, BLOCK)
+                g_banks[t, member] = g_bank
 
-            theta = results.tile([P, MEMBERS, C_THETA], F32)
-            nc.vector.tensor_tensor(out=theta[:], in0=theta_bank[:], in1=bias_theta, op=ALU.add)
+        thetas = {}
+        pooleds = {}
+
+        def copy_first_member(t):
+            pooled = results.tile([P, C_G + C_PHI], F32, name="pooled")
+            nc.scalar.copy(out=pooled[:, 0:C_G], in_=g_banks[t, 0][:])
+            pooleds[t] = pooled
+
+        def add_theta_bias(t):
+            theta = results.tile([P, MEMBERS, C_THETA], F32, name="theta")
+            nc.vector.tensor_tensor(
+                out=theta[:], in0=theta_banks[t][:], in1=bias_theta, op=ALU.add
+            )
+            thetas[t] = theta
+
+        def tanh_theta_store(t):
+            theta = thetas[t]
             nc.scalar.activation(out=theta[:], in_=theta[:], func=ACT.Tanh)
             for b in range(WINDOW_COLS):
                 nc.sync.dma_start(
@@ -207,40 +242,56 @@ def tile_selfattention3d_pb_kernel(
                     in_=theta[b:P:WINDOW_COLS, :, :].rearrange("a (di dj) c -> a di (dj c)", di=2),
                 )
 
-            pooled = results.tile([P, C_G + C_PHI], F32)
-            phi_halves = results.tile([P, 2, C_PHI], F32)
-            nc.scalar.copy(out=phi_halves[:], in_=phi_bank[:, 0:2, :])
-            nc.vector.tensor_tensor(
-                out=phi_halves[:], in0=phi_bank[:, 2:4, :], in1=phi_halves[:], op=ALU.max
+        def pool_phi(t):
+            nc.vector.tensor_reduce(
+                out=pooleds[t][:, C_G:],
+                in_=phi_banks[t][:].rearrange("p m c -> p c m"),
+                axis=mybir.AxisListType.X,
+                op=ALU.max,
             )
-            for member in range(MEMBERS):
-                g_bank = psum.tile([P, C_G], F32, tag="bank")
-                product(g_bank[:], x_codes, x_scales, member, g_codes, g_scales, 0, C_G)
-                if member == 0:
-                    nc.scalar.copy(out=pooled[:, 0:C_G], in_=g_bank[:])
-                else:
-                    nc.vector.tensor_tensor(
-                        out=pooled[:, 0:C_G], in0=g_bank[:], in1=pooled[:, 0:C_G], op=ALU.max
-                    )
+
+        def max_g(t, member):
             nc.vector.tensor_tensor(
-                out=pooled[:, C_G:], in0=phi_halves[:, 0, :], in1=phi_halves[:, 1, :], op=ALU.max
+                out=pooleds[t][:, 0:C_G],
+                in0=g_banks[t, member][:],
+                in1=pooleds[t][:, 0:C_G],
+                op=ALU.max,
             )
-            nc.vector.tensor_tensor(
-                out=pooled[:], in0=pooled[:], in1=bias[:, 0 : C_G + C_PHI], op=ALU.add
-            )
+
+        def add_pooled_bias_store(t):
+            pooled = pooleds[t]
+            adder = nc.vector if t == CHUNKS - 1 else nc.gpsimd
+            for columns in (slice(C_G, C_G + C_PHI), slice(0, C_G)):
+                adder.tensor_tensor(
+                    out=pooled[:, columns], in0=pooled[:, columns], in1=bias[:, columns], op=ALU.add
+                )
             nc.sync.dma_start(out=g_rows[t], in_=pooled[:, 0:C_G])
-            phi = results.tile([P, C_PHI], F32)
-            nc.scalar.activation(out=phi[:], in_=pooled[:, C_G:], func=ACT.Tanh)
+
+        def tanh_phi_store(t):
+            phi = results.tile([P, C_PHI], F32, name="phi")
+            nc.scalar.activation(out=phi[:], in_=pooleds[t][:, C_G:], func=ACT.Tanh)
             nc.sync.dma_start(out=phi_rows[t], in_=phi[:])
 
-        groupeds = [regroup(0)]
-        small_codes, small_scales = quantise_weights(4, 2)
-        g_codes, g_scales = quantise_weights(0, 4)
-        groupeds.append(regroup(1))
-        quantised = [quantise(groupeds[0])]
+        regroup(0)
+        regroup(1)
+        quantise(0, 0)
+        quantise(0, 1)
+        w_small = prepare_weights(4)
+        w_g_low = prepare_weights(0)
+        w_g_high = prepare_weights(2)
+        products(0)
         for t in range(CHUNKS):
-            if t + 2 < CHUNKS:
-                groupeds.append(regroup(t + 2))
-            if t + 1 < CHUNKS:
-                quantised.append(quantise(groupeds[t + 1]))
-            convolve_pool_store(t, quantised[t][0], quantised[t][1])
+            regroup(PASSES * t + 2)
+            regroup(PASSES * t + 3)
+            quantise(t + 1, 0)
+            quantise(t + 1, 1)
+            products(t + 1)
+            copy_first_member(t)
+            add_theta_bias(t)
+            pool_phi(t)
+            max_g(t, 1)
+            tanh_theta_store(t)
+            max_g(t, 2)
+            max_g(t, 3)
+            add_pooled_bias_store(t)
+            tanh_phi_store(t)

@@ -123,16 +123,17 @@ def tile_selfattention3d_pb_kernel(
             by_member = raws[t][:, c, :, :].rearrange(
                 "p k (a di b dj) -> p di dj a b k", a=WINDOW_ROWS, di=2, b=WINDOW_COLS, dj=2
             )
+            vector_rows = 2 if t == 0 else (1 if t < CHUNKS - 1 else 0)
             for di in range(2):
-                if di == 0:
+                if di < vector_rows:
                     nc.vector.tensor_copy(
-                        out=groupeds[t][:, c, 0:2, :, :].rearrange(
+                        out=groupeds[t][:, c, 2 * di : 2 * di + 2, :, :].rearrange(
                             "p dj (a b) k -> p a b k dj", a=WINDOW_ROWS
                         ),
                         in_=raws[t][:, c, :, :].rearrange(
                             "p k (a di b dj) -> p di a b k dj",
                             a=WINDOW_ROWS, di=2, b=WINDOW_COLS, dj=2,
-                        )[:, 0],
+                        )[:, di],
                     )
                 else:
                     for dj in range(2):
@@ -280,13 +281,15 @@ def tile_selfattention3d_pb_kernel(
         w_g_low = prepare_weights(0)
         w_g_high = prepare_weights(2)
         products(0)
+        regroup(2)
+        regroup(3)
         for t in range(CHUNKS):
-            regroup(PASSES * t + 2)
-            regroup(PASSES * t + 3)
             quantise(t + 1, 0)
             quantise(t + 1, 1)
             products(t + 1)
             copy_first_member(t)
+            regroup(PASSES * t + 4)
+            regroup(PASSES * t + 5)
             add_theta_bias(t)
             pool_phi(t)
             max_g(t, 1)

@@ -40,10 +40,7 @@ def tile_selfattention3d_pb_kernel(
     x_pieces = x.rearrange(
         "o (s p e) f i j -> (o s) p e (f i j)", s=PASSES * HALVES, p=P, e=PAIR
     )
-    theta_rows = out_0.rearrange(
-        "o (t a di b dj) c -> (o t) b a di (dj c)",
-        t=CHUNKS, a=WINDOW_ROWS, di=2, b=WINDOW_COLS, dj=2,
-    )
+    theta_rows = out_0.rearrange("o (t j p) c -> (o t) p j c", t=CHUNKS, p=P)
     phi_rows = out_1.rearrange("o (t w) c -> (o t) w c", t=CHUNKS)
     g_rows = out_2.rearrange("o (t w) c -> (o t) w c", t=CHUNKS)
     w_g_tiles = w_g.rearrange("(r p) k -> p r k", p=P)
@@ -103,8 +100,8 @@ def tile_selfattention3d_pb_kernel(
         )
         ones = consts.tile([P, P], BF16)
         nc.vector.memset(ones[:], 1.0)
-        bias = consts.tile([P, C_G + C_PHI + C_THETA], F32)
-        for first, width in ((0, C_G), (C_G, C_PHI + C_THETA)):
+        bias = consts.tile([P, C_G + C_PHI], F32)
+        for first, width in ((0, C_G), (C_G, C_PHI)):
             bias_bank = psum.tile([P, BANK], F32, tag="bank")
             nc.tensor.matmul(
                 out=bias_bank[:, 0:width],
@@ -114,7 +111,16 @@ def tile_selfattention3d_pb_kernel(
                 stop=True,
             )
             nc.scalar.copy(out=bias[:, first : first + width], in_=bias_bank[:, 0:width])
-        bias_theta = bias[:, C_G + C_PHI :].unsqueeze(1).to_broadcast([P, MEMBERS, C_THETA])
+        bias_theta_bank = psum.tile([P, BANK], F32, tag="bank")
+        nc.tensor.matmul(
+            out=bias_theta_bank[:, 0:P],
+            lhsT=bias_rows[:, C_G + C_PHI :],
+            rhs=ones[:],
+            start=True,
+            stop=True,
+        )
+        bias_theta = consts.tile([P, 1], F32)
+        nc.scalar.copy(out=bias_theta[:], in_=bias_theta_bank[:, 0:1])
 
         def regroup(q):
             t, c = divmod(q, PASSES)
@@ -123,17 +129,16 @@ def tile_selfattention3d_pb_kernel(
             by_member = raws[t][:, c, :, :].rearrange(
                 "p k (a di b dj) -> p di dj a b k", a=WINDOW_ROWS, di=2, b=WINDOW_COLS, dj=2
             )
-            vector_rows = 2 if t == 0 else (1 if t < CHUNKS - 1 else 0)
             for di in range(2):
-                if di < vector_rows:
+                if di == 0:
                     nc.vector.tensor_copy(
-                        out=groupeds[t][:, c, 2 * di : 2 * di + 2, :, :].rearrange(
+                        out=groupeds[t][:, c, 0:2, :, :].rearrange(
                             "p dj (a b) k -> p a b k dj", a=WINDOW_ROWS
                         ),
                         in_=raws[t][:, c, :, :].rearrange(
                             "p k (a di b dj) -> p di a b k dj",
                             a=WINDOW_ROWS, di=2, b=WINDOW_COLS, dj=2,
-                        )[:, di],
+                        )[:, 0],
                     )
                 else:
                     for dj in range(2):
@@ -205,9 +210,18 @@ def tile_selfattention3d_pb_kernel(
         def products(t):
             if t >= CHUNKS:
                 return
-            theta_bank = psum.tile([P, MEMBERS, C_THETA], F32, tag="bank")
-            for member in range(MEMBERS):
-                product(theta_bank[:, member, :], t, member, w_small, C_PHI, C_THETA)
+            w_codes, w_scales = w_small
+            theta_bank = psum.tile([P, MEMBERS * P], F32, tag="bank")
+            for c in range(PASSES):
+                nc.tensor.matmul_mx(
+                    out=theta_bank[:],
+                    lhsT=w_codes[:, c, C_PHI : C_PHI + C_THETA].bitcast(FP8X4),
+                    lhsT_scale=w_scales[:, c, C_PHI : C_PHI + C_THETA],
+                    rhs=x_codes[t][:, c, :, :].rearrange("p m w -> p (m w)").bitcast(FP8X4),
+                    rhs_scale=x_scales[t][:, c, :, :].rearrange("p m w -> p (m w)"),
+                    start=(c == 0),
+                    stop=(c == PASSES - 1),
+                )
             theta_banks[t] = theta_bank
             phi_bank = psum.tile([P, MEMBERS, C_PHI], F32, tag="bank")
             for member in range(MEMBERS):
@@ -219,7 +233,6 @@ def tile_selfattention3d_pb_kernel(
                 product(g_bank[:, BLOCK:C_G], t, member, w_g_high, 0, BLOCK)
                 g_banks[t, member] = g_bank
 
-        thetas = {}
         pooleds = {}
 
         def copy_first_member(t):
@@ -227,21 +240,26 @@ def tile_selfattention3d_pb_kernel(
             nc.scalar.copy(out=pooled[:, 0:C_G], in_=g_banks[t, 0][:])
             pooleds[t] = pooled
 
-        def add_theta_bias(t):
-            theta = results.tile([P, MEMBERS, C_THETA], F32, name="theta")
-            nc.vector.tensor_tensor(
-                out=theta[:], in0=theta_banks[t][:], in1=bias_theta, op=ALU.add
-            )
-            thetas[t] = theta
-
         def tanh_theta_store(t):
-            theta = thetas[t]
-            nc.scalar.activation(out=theta[:], in_=theta[:], func=ACT.Tanh)
-            for b in range(WINDOW_COLS):
-                nc.sync.dma_start(
-                    out=theta_rows[t, b],
-                    in_=theta[b:P:WINDOW_COLS, :, :].rearrange("a (di dj) c -> a di (dj c)", di=2),
+            by_channel = results.tile([P, CHUNK], F32, name="theta_by_channel")
+            for di in range(2):
+                nc.scalar.activation(
+                    out=by_channel[:].rearrange(
+                        "p (a di b dj) -> p di a b dj", a=WINDOW_ROWS, di=2, b=WINDOW_COLS, dj=2
+                    )[:, di],
+                    in_=theta_banks[t][:].rearrange(
+                        "p (di dj a b) -> p di a b dj", di=2, dj=2, a=WINDOW_ROWS, b=WINDOW_COLS
+                    )[:, di],
+                    func=ACT.Tanh,
+                    bias=bias_theta[:],
+                    scale=1.0,
                 )
+            flipped = psum.tile([P, CHUNK // P, C_THETA], F32, tag="bank")
+            for j in range(CHUNK // P):
+                nc.tensor.transpose(flipped[:, j, :], by_channel[:, j * P : (j + 1) * P], ident[:])
+            theta = results.tile([P, CHUNK // P, C_THETA], F32, name="theta")
+            nc.scalar.copy(out=theta[:], in_=flipped[:])
+            nc.sync.dma_start(out=theta_rows[t], in_=theta[:])
 
         def pool_phi(t):
             nc.vector.tensor_reduce(
@@ -281,19 +299,16 @@ def tile_selfattention3d_pb_kernel(
         w_g_low = prepare_weights(0)
         w_g_high = prepare_weights(2)
         products(0)
-        regroup(2)
-        regroup(3)
         for t in range(CHUNKS):
+            regroup(PASSES * t + 2)
+            regroup(PASSES * t + 3)
             quantise(t + 1, 0)
             quantise(t + 1, 1)
             products(t + 1)
             copy_first_member(t)
-            regroup(PASSES * t + 4)
-            regroup(PASSES * t + 5)
-            add_theta_bias(t)
+            tanh_theta_store(t)
             pool_phi(t)
             max_g(t, 1)
-            tanh_theta_store(t)
             max_g(t, 2)
             max_g(t, 3)
             add_pooled_bias_store(t)

from contextlib import ExitStack

import concourse.mybir as mybir
from concourse.masks import make_identity

FLOPS = 2 * (128 + 128 + 512) * 1024 * 2048

BF16 = mybir.dt.bfloat16
F32 = mybir.dt.float32
U32 = mybir.dt.uint32
U8 = mybir.dt.uint8
FP8X4 = mybir.dt.float8_e4m3fn_x4
ALU = mybir.AluOpType
ACT = mybir.ActivationFunctionType

P = 128
PACK = 4
PASSES = 2
HALVES = 2
PAIR = 2
CHANNELS = 1024
CHUNKS = 4
CHUNK = 512
WINDOW_ROWS = 16
WINDOW_COLS = 8
MEMBERS = 4
C_G = 512
C_PHI = 128
C_THETA = 128
BLOCK = 256
BANK = 512
PSUM_BANKS = 8


def tile_selfattention3d_pb_kernel(
    tc, x, w_theta, b_theta, w_phi, b_phi, w_g, b_g, out_0, out_1, out_2
):
    nc = tc.nc

    x_pieces = x.rearrange(
        "o (s p e) f i j -> (o s) p e (f i j)", s=PASSES * HALVES, p=P, e=PAIR
    )
    theta_rows = out_0.rearrange("o (t j p) c -> (o t) p j c", t=CHUNKS, p=P)
    phi_rows = out_1.rearrange("o (t w) c -> (o t) w c", t=CHUNKS)
    g_rows = out_2.rearrange("o (t w) c -> (o t) w c", t=CHUNKS)
    w_g_tiles = w_g.rearrange("(r p) k -> p r k", p=P)

    with ExitStack() as ctx:
        consts = ctx.enter_context(tc.tile_pool(name="consts", bufs=1))
        per_chunk = ctx.enter_context(tc.tile_pool(name="per_chunk", bufs=CHUNKS))
        results = ctx.enter_context(tc.tile_pool(name="results", bufs=CHUNKS))
        psum = ctx.enter_context(tc.psum_pool(name="psum", bufs=PSUM_BANKS))

        raws = [per_chunk.tile([P, PASSES, PACK, CHUNK], BF16, name="raw") for t in range(CHUNKS)]
        groupeds = [
            per_chunk.tile([P, PASSES, MEMBERS, P, PACK], BF16, align_bytes=64, name="grouped")
            for t in range(CHUNKS)
        ]
        x_codes = [
            per_chunk.tile([P, PASSES, MEMBERS, P], U32, align_bytes=64, name="x_codes")
            for t in range(CHUNKS)
        ]
        x_scales = [
            per_chunk.tile([P, PASSES, MEMBERS, P], U8, align_bytes=64, name="x_scales")
            for t in range(CHUNKS)
        ]

        def load_chunk(t):
            for c in range(PASSES):
                for u in range(HALVES):
                    nc.sync.dma_start(
                        out=raws[t][:, c, PAIR * u : PAIR * (u + 1), :],
                        in_=x_pieces[HALVES * c + u, :, :, t * CHUNK : (t + 1) * CHUNK],
                    )

        w_rows = consts.tile([P, 6, CHANNELS], BF16)
        load_chunk(0)
        nc.sync.dma_start(out=w_rows[:, 4, :], in_=w_phi)
        nc.sync.dma_start(out=w_rows[:, 5, :], in_=w_theta)
        nc.sync.dma_start(out=w_rows[:, 0:2, :], in_=w_g_tiles[:, 0:2, :])
        nc.sync.dma_start(out=w_rows[:, 2:4, :], in_=w_g_tiles[:, 2:4, :])
        for t in range(1, CHUNKS):
            load_chunk(t)

        warm = consts.tile([P, 1], F32)
        nc.vector.memset(warm[:], 0.0)
        nc.scalar.activation(out=warm[:], in_=warm[:], func=ACT.Tanh)

        ident = consts.tile([P, P], F32)
        make_identity(nc, ident[:])

        bias_rows = consts.tile([P, C_G + C_PHI + C_THETA], BF16)
        nc.vector.memset(bias_rows[:], 0.0)
        nc.scalar.dma_start(out=bias_rows[0:1, 0:C_G], in_=b_g.rearrange("(o n) -> o n", o=1))
        nc.scalar.dma_start(
            out=bias_rows[0:1, C_G : C_G + C_PHI], in_=b_phi.rearrange("(o n) -> o n", o=1)
        )
        nc.scalar.dma_start(
            out=bias_rows[0:1, C_G + C_PHI :], in_=b_theta.rearrange("(o n) -> o n", o=1)
        )
        ones = consts.tile([P, P], BF16)
        nc.vector.memset(ones[:], 1.0)
        bias = consts.tile([P, C_G + C_PHI], F32)
        for first, width in ((0, C_G), (C_G, C_PHI)):
            bias_bank = psum.tile([P, BANK], F32, tag="bank")
            nc.tensor.matmul(
                out=bias_bank[:, 0:width],
                lhsT=ones[:],
                rhs=bias_rows[:, first : first + width],
                start=True,
                stop=True,
            )
            nc.scalar.copy(out=bias[:, first : first + width], in_=bias_bank[:, 0:width])
        bias_theta_bank = psum.tile([P, BANK], F32, tag="bank")
        nc.tensor.matmul(
            out=bias_theta_bank[:, 0:P],
            lhsT=bias_rows[:, C_G + C_PHI :],
            rhs=ones[:],
            start=True,
            stop=True,
        )
        bias_theta = consts.tile([P, 1], F32)
        nc.scalar.copy(out=bias_theta[:], in_=bias_theta_bank[:, 0:1])

        def regroup(q):
            t, c = divmod(q, PASSES)
            if t >= CHUNKS:
                return
            by_member = raws[t][:, c, :, :].rearrange(
                "p k (a di b dj) -> p di dj a b k", a=WINDOW_ROWS, di=2, b=WINDOW_COLS, dj=2
            )
            for di in range(2):
                if di == 0:
                    nc.vector.tensor_copy(
                        out=groupeds[t][:, c, 0:2, :, :].rearrange(
                            "p dj (a b) k -> p a b k dj", a=WINDOW_ROWS
                        ),
                        in_=raws[t][:, c, :, :].rearrange(
                            "p k (a di b dj) -> p di a b k dj",
                            a=WINDOW_ROWS, di=2, b=WINDOW_COLS, dj=2,
                        )[:, 0],
                    )
                else:
                    for dj in range(2):
                        nc.scalar.copy(
                            out=groupeds[t][:, c, 2 * di + dj, :, :].rearrange(
                                "p (a b) k -> p a b k", a=WINDOW_ROWS
                            ),
                            in_=by_member[:, di, dj],
                        )

        def quantise(t, c):
            if t >= CHUNKS:
                return
            nc.vector.quantize_mx(
                out=x_codes[t][:, c, :, :].rearrange("p m w -> p (m w)").bitcast(FP8X4),
                scales=x_scales[t][:, c, :, :].rearrange("p m w -> p (m w)"),
                in_=groupeds[t][:, c, :, :, :].rearrange("p m w k -> p (m w k)"),
            )

        def prepare_weights(first_row_tile):
            grouped = consts.tile(
                [P, PASSES, BLOCK * PACK], BF16, align_bytes=64,
                name="w_grouped%d" % first_row_tile,
            )
            for c in range(PASSES):
                w_bank = psum.tile([P, 2, HALVES, P], F32, tag="bank")
                for r in range(2):
                    words = w_rows[:, first_row_tile + r, :].bitcast(F32)
                    for u in range(HALVES):
                        first = (HALVES * c + u) * P
                        nc.tensor.transpose(
                            w_bank[:, r, u, :], words[:, first : first + P], ident[:]
                        )
                out_words = grouped[:, c, :].bitcast(F32).rearrange(
                    "p (r o u) -> p r o u", r=2, u=HALVES
                )
                in_words = w_bank[:].rearrange("p r u o -> p r o u")
                nc.scalar.copy(out=out_words, in_=in_words)
            codes = consts.tile(
                [P, PASSES, BLOCK], U32, align_bytes=64, name="w_codes%d" % first_row_tile
            )
            scales = consts.tile(
                [P, PASSES, BLOCK], U8, align_bytes=64, name="w_scales%d" % first_row_tile
            )
            nc.vector.quantize_mx(
                out=codes[:].rearrange("p c n -> p (c n)").bitcast(FP8X4),
                scales=scales[:].rearrange("p c n -> p (c n)"),
                in_=grouped[:].rearrange("p c n -> p (c n)"),
            )
            return codes, scales

        def product(out, t, member, weights, first, width):
            w_codes, w_scales = weights
            for c in range(PASSES):
                nc.tensor.matmul_mx(
                    out=out,
                    lhsT=x_codes[t][:, c, member, :].bitcast(FP8X4),
                    lhsT_scale=x_scales[t][:, c, member, :],
                    rhs=w_codes[:, c, first : first + width].bitcast(FP8X4),
                    rhs_scale=w_scales[:, c, first : first + width],
                    start=(c == 0),
                    stop=(c == PASSES - 1),
                )

        theta_banks = {}
        phi_banks = {}
        g_banks = {}

        def products(t):
            if t >= CHUNKS:
                return
            w_codes, w_scales = w_small
            theta_bank = psum.tile([P, MEMBERS * P], F32, tag="bank")
            for c in range(PASSES):
                nc.tensor.matmul_mx(
                    out=theta_bank[:],
                    lhsT=w_codes[:, c, C_PHI : C_PHI + C_THETA].bitcast(FP8X4),
                    lhsT_scale=w_scales[:, c, C_PHI : C_PHI + C_THETA],
                    rhs=x_codes[t][:, c, :, :].rearrange("p m w -> p (m w)").bitcast(FP8X4),
                    rhs_scale=x_scales[t][:, c, :, :].rearrange("p m w -> p (m w)"),
                    start=(c == 0),
                    stop=(c == PASSES - 1),
                )
            theta_banks[t] = theta_bank
            phi_bank = psum.tile([P, MEMBERS, C_PHI], F32, tag="bank")
            for member in range(MEMBERS):
                product(phi_bank[:, member, :], t, member, w_small, 0, C_PHI)
            phi_banks[t] = phi_bank
            for member in range(MEMBERS):
                g_bank = psum.tile([P, C_G], F32, tag="bank")
                product(g_bank[:, 0:BLOCK], t, member, w_g_low, 0, BLOCK)
                product(g_bank[:, BLOCK:C_G], t, member, w_g_high, 0, BLOCK)
                g_banks[t, member] = g_bank

        pooleds = {}

        def copy_first_member(t):
            pooled = results.tile([P, C_G + C_PHI], F32, name="pooled")
            nc.scalar.copy(out=pooled[:, 0:C_G], in_=g_banks[t, 0][:])
            pooleds[t] = pooled

        def tanh_theta_store(t):
            by_channel = results.tile([P, CHUNK], F32, name="theta_by_channel")
            for di in range(2):
                nc.scalar.activation(
                    out=by_channel[:].rearrange(
                        "p (a di b dj) -> p di a b dj", a=WINDOW_ROWS, di=2, b=WINDOW_COLS, dj=2
                    )[:, di],
                    in_=theta_banks[t][:].rearrange(
                        "p (di dj a b) -> p di a b dj", di=2, dj=2, a=WINDOW_ROWS, b=WINDOW_COLS
                    )[:, di],
                    func=ACT.Tanh,
                    bias=bias_theta[:],
                    scale=1.0,
                )
            flipped = psum.tile([P, CHUNK // P, C_THETA], F32, tag="bank")
            for j in range(CHUNK // P):
                nc.tensor.transpose(flipped[:, j, :], by_channel[:, j * P : (j + 1) * P], ident[:])
            theta = results.tile([P, CHUNK // P, C_THETA], F32, name="theta")
            nc.scalar.copy(out=theta[:], in_=flipped[:])
            nc.sync.dma_start(out=theta_rows[t], in_=theta[:])

        def pool_phi(t):
            nc.vector.tensor_reduce(
                out=pooleds[t][:, C_G:],
                in_=phi_banks[t][:].rearrange("p m c -> p c m"),
                axis=mybir.AxisListType.X,
                op=ALU.max,
            )

        def max_g(t, member):
            nc.vector.tensor_tensor(
                out=pooleds[t][:, 0:C_G],
                in0=g_banks[t, member][:],
                in1=pooleds[t][:, 0:C_G],
                op=ALU.max,
            )

        def add_pooled_bias_store(t):
            pooled = pooleds[t]
            adder = nc.vector if t == CHUNKS - 1 else nc.gpsimd
            for columns in (slice(C_G, C_G + C_PHI), slice(0, C_G)):
                adder.tensor_tensor(
                    out=pooled[:, columns], in0=pooled[:, columns], in1=bias[:, columns], op=ALU.add
                )
            nc.sync.dma_start(out=g_rows[t], in_=pooled[:, 0:C_G])

        def tanh_phi_store(t):
            phi = results.tile([P, C_PHI], F32, name="phi")
            nc.scalar.activation(out=phi[:], in_=pooleds[t][:, C_G:], func=ACT.Tanh)
            nc.sync.dma_start(out=phi_rows[t], in_=phi[:])

        regroup(0)
        regroup(1)
        quantise(0, 0)
        quantise(0, 1)
        w_small = prepare_weights(4)
        w_g_low = prepare_weights(0)
        w_g_high = prepare_weights(2)
        products(0)
        for t in range(CHUNKS):
            regroup(PASSES * t + 2)
            regroup(PASSES * t + 3)
            quantise(t + 1, 0)
            quantise(t + 1, 1)
            products(t + 1)
            copy_first_member(t)
            tanh_theta_store(t)
            pool_phi(t)
            max_g(t, 1)
            max_g(t, 2)
            max_g(t, 3)
            add_pooled_bias_store(t)
            tanh_phi_store(t)
